import numpy as np
import ml_dtypes


def mxq(x, axis, fmt="e4m3"):
    dtype, down = {"e4m3": (ml_dtypes.float8_e4m3fn, 7), "e5m2": (ml_dtypes.float8_e5m2, 14)}[fmt]
    v = np.moveaxis(np.asarray(x, np.float32).astype(ml_dtypes.bfloat16).astype(np.float64), axis, -1)
    blocks = v.reshape(v.shape[:-1] + (-1, 32))
    amax = np.abs(blocks).max(-1, keepdims=True)
    byte = np.maximum(np.where(amax > 0, np.frexp(amax)[1] - 1 + 127, 0) - down, 1)
    scale = np.exp2(byte - 127.0)
    codes = (blocks / scale).astype(np.float32).astype(dtype).astype(np.float64)
    return np.moveaxis((codes * scale).reshape(v.shape), -1, axis)


WIDE = False


def mx_kscale(k):
    if not WIDE:
        return np.ones(k)
    levels = np.array([10, -10, 5, -5, 0])
    a = np.random.permutation(np.resize(levels, k // 512 * 4)).reshape(k // 512, 4)
    idx = np.arange(k)
    return np.exp2(a[idx // 512, idx % 128 // 32])


BF16 = ml_dtypes.bfloat16


def bf(x):
    return np.asarray(x, np.float32).astype(BF16)


def f64(x):
    return np.asarray(x).astype(np.float64)


B, S, HIDDEN, N_HEADS, N_KV, HD, QB = 1, 512, 2560, 20, 5, 128, 512
QD = N_HEADS * HD
KD = N_KV * HD


def apply_rope(t, cos_f, sin_f):
    n = t.shape[1]
    cos = cos_f[:n][None, :, None, :]
    sin = sin_f[:n][None, :, None, :]
    half = t.shape[-1] // 2
    t1, t2 = t[..., :half], t[..., half:]
    return t * cos + np.concatenate([-t2, t1], axis=-1) * sin


def setup_inputs():
    s = mx_kscale(HIDDEN)
    a = 1.0 / np.sqrt(HIDDEN)
    return {"x": bf(np.random.standard_normal((B, S, HIDDEN)) * s),
            "cos_f": bf(np.random.uniform(size=(S, HD))),
            "sin_f": bf(np.random.uniform(size=(S, HD))),
            "Wq": bf(np.random.standard_normal((HIDDEN, QD)) * 2.0 * a / s[:, None]),
            "Wk": bf(np.random.standard_normal((HIDDEN, KD)) * 2.0 * a / s[:, None]),
            "Wv": bf(np.random.standard_normal((HIDDEN, KD)) * a / s[:, None])}


def reference(x, cos_f, sin_f, Wq, Wk, Wv):
    xq = mxq(f64(x), 2, "e4m3")
    q = (xq @ mxq(f64(Wq), 0, "e4m3")).reshape(B, S, N_HEADS, HD)
    k = (xq @ mxq(f64(Wk), 0, "e4m3")).reshape(B, S, N_KV, HD)
    v = (xq @ mxq(f64(Wv), 0, "e4m3")).reshape(B, S, N_KV, HD)
    return apply_rope(q, f64(cos_f), f64(sin_f)), apply_rope(k, f64(cos_f), f64(sin_f)), v

@@ -1,0 +1,278 @@
+from contextlib import ExitStack
+
+import concourse.mybir as mybir
+from concourse.masks import make_identity
+
+F32 = mybir.dt.float32
+BF16 = mybir.dt.bfloat16
+U32 = mybir.dt.uint32
+U8 = mybir.dt.uint8
+FP8X4 = mybir.dt.float8_e4m3fn_x4
+MULT = mybir.AluOpType.mult
+ADD = mybir.AluOpType.add
+
+P = 128
+TOK = 512
+HID = 2560
+HD = 128
+NT = TOK // P
+NG = HID // 512
+FLOPS = 2 * TOK * HID * 3840
+
+WIDTH = {"K": 512, "Qa": 1024, "Qb": 1024, "Qc": 512, "V": 512}
+SPLIT = {"K": [344, 360, 360, 264, 264], "Qa": [704, 704, 712, 712, 704], "Qb": [800, 888, 904, 888, 888],
+         "Qc": [488, 512, 512, 512, 512], "V": [512, 512, 512, 512, 512]}
+TAIL_ON_SCALAR = {"Kt": 3, "Vt": 5}
+X_ON_SCALAR = [3, 3]
+ROPES = {"K": [0, 0, 0, 0, 0], "Kt": [0], "x": [0, 0], "Qa": [0, 1, 1, 1, 1], "Qb": [1, 2, 2, 2, 2], "Qc": [0, 2, 2, 2, 2], "Vt": [0], "V": [1, 2, 1, 0, 0]}
+START = [("w", "K", 0), ("w", "K", 1), ("x", "x", 0), ("w", "K", 2), ("x", "x", 1), ("w", "K", 3), ("w", "K", 4), ("t", "Kt", 0)]
+VECTOR_ADDS = []
+RAW_BUFS = 10
+GRP_BUFS = 3
+OUT_BUFS = 3
+PROD_BUFS = 3
+
+
+def tile_gqattention_pa_kernel(tc, x, cos_f, sin_f, Wq, Wk, Wv, out_0, out_1, out_2):
+    nc = tc.nc
+    x2 = x.flatten_outer_dims().rearrange("(p t) k -> p t k", t=NT)
+    oq = out_0.rearrange("b s h d -> (b s) (h d)").rearrange("(p t) c -> p t c", t=NT)
+    ok = out_1.rearrange("b s h d -> (b s) (h d)").rearrange("(p t) c -> p t c", t=NT)
+    ov = out_2.rearrange("b s h d -> (b s) (h d)").rearrange("(p t) c -> p t c", t=NT)
+    source = {"K": (Wk, 0, 640), "Qa": (Wq, 0, 1024), "Qb": (Wq, 1024, 1024), "Qc": (Wq, 2048, 512), "V": (Wv, 0, 640)}
+
+    items = list(START)
+    for key in ("Qa", "Qb", "Qc"):
+        items.extend([("w", key, g) for g in range(NG)])
+    items.append(("t", "Vt", 0))
+    items.extend([("w", "V", g) for g in range(NG)])
+
+    with ExitStack() as ctx:
+        const = ctx.enter_context(tc.tile_pool(name="const", bufs=1))
+        rawp = ctx.enter_context(tc.tile_pool(name="rawp", bufs=RAW_BUFS))
+        grpp = ctx.enter_context(tc.tile_pool(name="grpp", bufs=GRP_BUFS))
+        codep = ctx.enter_context(tc.tile_pool(name="codep", bufs=2))
+        prodp = ctx.enter_context(tc.tile_pool(name="prodp", bufs=PROD_BUFS))
+        outp = ctx.enter_context(tc.tile_pool(name="outp", bufs=OUT_BUFS))
+        psum = ctx.enter_context(tc.psum_pool(name="psum", bufs=8))
+        ctx.enter_context(tc.manual_schedule())
+
+        raws = {}
+        loads = []
+        for kind, key, g in items:
+            if kind == "x":
+                loads.extend([("x", 2 * g), ("x", 2 * g + 1)])
+            elif kind == "w":
+                loads.append((key, g))
+        count = {"load": 0, "rope": 0}
+
+        def issue(n):
+            for i in range(count["load"], min(count["load"] + n, len(loads))):
+                key, g = loads[i]
+                if key == "x":
+                    t = rawp.tile([P, HID], BF16, name="xraw", tag="raw")
+                    nc.sync.dma_start(out=t[:], in_=x2[:, g, :])
+                else:
+                    src, c0, w = source[key]
+                    t = rawp.tile([P, 4, w], BF16, name="raw", tag="raw")
+                    nc.sync.dma_start(out=t[:], in_=src[512 * g:512 * (g + 1), c0:c0 + w].rearrange("(p t) c -> p t c", t=4))
+                raws[key, g] = t
+            count["load"] = min(count["load"] + n, len(loads))
+
+        ident = const.tile([P, P], F32, name="ident")
+        make_identity(nc, ident[:])
+        cs = const.tile([P, 2, NT, HD], BF16, name="cs")
+        tab = const.tile([P, NT, 2, HD], F32, name="tab")
+        xc = const.tile([P, 2, NG, 256], U32, name="xc", align_bytes=64)
+        xs = const.tile([P, 2, NG, 256], U8, name="xs", align_bytes=64)
+
+        def tables():
+            nc.scalar.dma_start(out=cs[:, 0], in_=cos_f.rearrange("(p t) d -> p t d", t=NT))
+            nc.scalar.dma_start(out=cs[:, 1], in_=sin_f.rearrange("(p t) d -> p t d", t=NT))
+            nc.gpsimd.tensor_scalar(out=tab[:, :, 0, :], in0=cs[:, 0], scalar1=1.0, scalar2=0.0, op0=MULT, op1=ADD)
+            nc.gpsimd.tensor_scalar(out=tab[:, :, 1, 0:64], in0=cs[:, 1, :, 64:128], scalar1=1.0, scalar2=0.0, op0=MULT, op1=ADD)
+            nc.gpsimd.tensor_scalar(out=tab[:, :, 1, 64:128], in0=cs[:, 1, :, 0:64], scalar1=-1.0, scalar2=0.0, op0=MULT, op1=ADD)
+
+        def regroup(on_scalar, dst, src):
+            d = dst.rearrange("p (c i) t -> p c t i", i=4)
+            s = src.rearrange("p t (c i) -> p c t i", i=4)
+            if on_scalar:
+                nc.scalar.copy(out=d, in_=s)
+            else:
+                nc.vector.tensor_copy(out=d, in_=s)
+
+        codes = {}
+        grouped = {}
+
+        def copy_item(kind, key, g):
+            if kind == "w":
+                w = WIDTH[key]
+                if g == 0:
+                    wc = codep.tile([P, NG, w], U32, name="wc", tag="wc", align_bytes=64)
+                    ws = codep.tile([P, NG, w], U8, name="ws", tag="ws", align_bytes=64)
+                    codes[key] = (wc, ws)
+                grp = grpp.tile([P, w, 4], BF16, name="grp", tag="grp", align_bytes=64)
+                c = SPLIT[key][g]
+                raw = raws[key, g]
+                regroup(True, grp[:, 0:c, :], raw[:, :, 0:c])
+                if c < w:
+                    regroup(False, grp[:, c:w, :], raw[:, :, c:w])
+            elif kind == "t":
+                wc = codep.tile([P, NG, HD], U32, name="tc", tag="tc", align_bytes=64)
+                ws = codep.tile([P, NG, HD], U8, name="tsc", tag="tsc", align_bytes=64)
+                codes[key] = (wc, ws)
+                grp = grpp.tile([P, NG, HD, 4], BF16, name="grp", tag="grp", align_bytes=64)
+                for gg in range(NG):
+                    regroup(gg < TAIL_ON_SCALAR[key], grp[:, gg], raws[key[0], gg][:, :, 512:640])
+            else:
+                grp = prodp.tile([P, NG, 256, 4], BF16, name="xg", tag="pr", align_bytes=64)
+                for gg in range(NG):
+                    xt = psum.tile([P, 2, 256], F32, name="xt", tag="ps")
+                    for u in range(2):
+                        for j in range(2):
+                            xw = raws["x", 2 * g + j][:].bitcast(F32)
+                            nc.tensor.transpose(out=xt[:, u, P * j:P * (j + 1)], in_=xw[:, 256 * gg + u:256 * (gg + 1):2],
+                                                identity=ident[:])
+                    dst = grp[:, gg].rearrange("p s t -> p (s t)").bitcast(F32).rearrange("p (s u) -> p s u", u=2)
+                    src = xt[:].rearrange("p u s -> p s u")
+                    if gg % 2 == 0 and gg // 2 < X_ON_SCALAR[g]:
+                        nc.scalar.copy(out=dst, in_=src)
+                    else:
+                        nc.vector.tensor_copy(out=dst, in_=src)
+            grouped[key, g] = grp
+
+        def quant5(dst_c, dst_s, src):
+            nc.vector.quantize_mx(out=dst_c[:, 0:4, :].rearrange("p g c -> p (g c)").bitcast(FP8X4),
+                                  scales=dst_s[:, 0:4, :].rearrange("p g c -> p (g c)"),
+                                  in_=src[:, 0:4].rearrange("p g c t -> p (g c t)"))
+            nc.vector.quantize_mx(out=dst_c[:, 4, :].bitcast(FP8X4), scales=dst_s[:, 4, :],
+                                  in_=src[:, 4].rearrange("p c t -> p (c t)"))
+
+        def quant_item(kind, key, g):
+            if kind == "w":
+                wc, ws = codes[key]
+                nc.vector.quantize_mx(out=wc[:, g, :].bitcast(FP8X4), scales=ws[:, g, :],
+                                      in_=grouped[key, g][:].rearrange("p c t -> p (c t)"))
+            elif kind == "t":
+                quant5(codes[key][0], codes[key][1], grouped[key, g])
+            else:
+                quant5(xc[:, g], xs[:, g], grouped[key, g])
+
+        def mx(acc, key, g, t, c0, n):
+            wc, ws = codes[key]
+            tok = slice(P * (t % 2), P * (t % 2) + P)
+            nc.tensor.matmul_mx(out=acc, lhsT=xc[:, t // 2, g, tok].bitcast(FP8X4), lhsT_scale=xs[:, t // 2, g, tok],
+                                rhs=wc[:, g, c0:c0 + n].bitcast(FP8X4), rhs_scale=ws[:, g, c0:c0 + n],
+                                start=(g == 0), stop=(g == NG - 1))
+
+        units = []
+
+        def tab_of(t):
+            return tab[:, t].unsqueeze(2).to_broadcast([P, 2, 4, HD])
+
+        def pair_units(accs, dram, c0):
+            for t in (0, 2):
+                units.append(([accs[t], accs[t + 1]], [tab_of(t), tab_of(t + 1)], dram[:, t:t + 2, c0:c0 + 512]))
+
+        def mm_group(key, dram, c0):
+            accs = {}
+            nchunks = WIDTH[key] // 512
+            for t in range(NT):
+                for c in range(nchunks):
+                    acc = psum.tile([P, 512], F32, name="acc", tag="ps")
+                    accs[t, c] = acc
+                    for g in range(NG):
+                        mx(acc[:], key, g, t, 512 * c, 512)
+                if nchunks == 2:
+                    units.append(([accs[t, 0], accs[t, 1]], [tab_of(t), tab_of(t)],
+                                  dram[:, t, c0:c0 + 1024].rearrange("p (b c) -> p b c", b=2)))
+            if nchunks == 1:
+                pair_units([accs[t, 0] for t in range(NT)], dram, c0)
+
+        def mm_tail(key):
+            acc = psum.tile([P, 512], F32, name="acc", tag="ps")
+            for t in range(NT):
+                for g in range(NG):
+                    mx(acc[:, P * t:P * (t + 1)], key, g, t, 0, P)
+            return acc
+
+        open_acc = {}
+
+        def mm_pass(key, g):
+            if g == 0:
+                accs = []
+                for t in range(NT):
+                    acc = psum.tile([P, 512], F32, name="acc", tag="ps")
+                    accs.append(acc)
+                open_acc[key] = accs
+            for t in range(NT):
+                mx(open_acc[key][t][:], key, g, t, 0, 512)
+
+        live = {}
+
+        def rope_mults(n):
+            for i in range(n):
+                u, b = count["rope"] // 2, count["rope"] % 2
+                if u >= len(units):
+                    return
+                accs, tabs, dram = units[u]
+                nb = len(accs)
+                if b == 0:
+                    pr = prodp.tile([P, nb, 2, 4, HD], F32, name="pr", tag="pr", align_bytes=64)
+                    live["pr"] = pr
+                pr = live["pr"]
+                a4 = accs[b][:].rearrange("p (h d) -> p h d", d=HD).unsqueeze(1).to_broadcast([P, 2, 4, HD])
+                nc.vector.tensor_tensor(out=pr[:, b], in0=a4, in1=tabs[b], op=MULT)
+                count["rope"] += 1 if b + 1 < nb else 2 - b
+                if b + 1 == nb:
+                    o = outp.tile([P, nb, 4, HD], F32, name="o", tag="o")
+                    eng = nc.vector if u in VECTOR_ADDS else nc.gpsimd
+                    eng.tensor_tensor(out=o[:, :, :, 0:64], in0=pr[:, :, 0, :, 0:64], in1=pr[:, :, 1, :, 64:128], op=ADD)
+                    eng.tensor_tensor(out=o[:, :, :, 64:128], in0=pr[:, :, 0, :, 64:128], in1=pr[:, :, 1, :, 0:64], op=ADD)
+                    nc.sync.dma_start(out=dram, in_=o[:, 0] if nb == 1 else o[:].rearrange("p b h d -> p b (h d)"))
+
+        tables()
+        issue(RAW_BUFS)
+        done = set()
+        state = {"kpass": 0, "vt": None}
+
+        def after_quant(kind, key, g):
+            done.add((key, g))
+            x_ready = ("x", 0) in done and ("x", 1) in done
+            if x_ready:
+                for gg in range(state["kpass"], NG):
+                    if ("K", gg) in done and state["kpass"] == gg:
+                        mm_pass("K", gg)
+                        state["kpass"] = gg + 1
+                        if gg == NG - 1:
+                            pair_units(open_acc["K"], ok, 0)
+            if key == "Kt":
+                units.append(([mm_tail("Kt")], [tab[:].rearrange("p t r d -> p r t d")], ok[:, :, 512:640]))
+            if g == NG - 1 and key in ("Qa", "Qb", "Qc"):
+                mm_group(key, oq, source[key][1])
+            if key == "V":
+                mm_pass("V", g)
+                if g == 2:
+                    state["vt"] = mm_tail("Vt")
+
+        for i in range(len(items)):
+            kind, key, g = items[i]
+            copy_item(kind, key, g)
+            issue(2 if kind == "x" else 5 if key == "Kt" else 0 if kind == "t" or key in ("K", "V") else 1)
+            if i > 0:
+                quant_item(*items[i - 1])
+            rope_mults(ROPES[key][g])
+            if i > 0:
+                after_quant(*items[i - 1])
+        quant_item(*items[-1])
+        ot = outp.tile([P, 512], F32, name="o", tag="o")
+        nc.scalar.copy(out=ot[:], in_=state["vt"][:])
+        nc.sync.dma_start(out=ov[:, :, 512:640], in_=ot[:].rearrange("p (t c) -> p t c", c=P))
+        after_quant(*items[-1])
+        for t in range(NT):
+            o1 = outp.tile([P, 512], F32, name="o1", tag="o1", bufs=4)
+            if t % 2 == 0:
+                nc.scalar.copy(out=o1[:], in_=open_acc["V"][t][:])
+            else:
+                nc.vector.tensor_copy(out=o1[:], in_=open_acc["V"][t][:])
+            nc.sync.dma_start(out=ov[:, t, 0:512], in_=o1[:])

@@ -19,14 +19,13 @@ NT = TOK // P
 NG = HID // 512
 FLOPS = 2 * TOK * HID * 3840
 
-WIDTH = {"K": 512, "Qa": 1024, "Qb": 1024, "Qc": 512, "V": 512}
-SPLIT = {"K": [344, 360, 360, 264, 264], "Qa": [704, 704, 712, 712, 704], "Qb": [800, 888, 904, 888, 888],
-         "Qc": [488, 512, 512, 512, 512], "V": [512, 512, 512, 512, 512]}
-TAIL_ON_SCALAR = {"Kt": 3, "Vt": 5}
-X_ON_SCALAR = [3, 3]
-ROPES = {"K": [0, 0, 0, 0, 0], "Kt": [0], "x": [0, 0], "Qa": [0, 1, 1, 1, 1], "Qb": [1, 2, 2, 2, 2], "Qc": [0, 2, 2, 2, 2], "Vt": [0], "V": [1, 2, 1, 0, 0]}
-START = [("w", "K", 0), ("w", "K", 1), ("x", "x", 0), ("w", "K", 2), ("x", "x", 1), ("w", "K", 3), ("w", "K", 4), ("t", "Kt", 0)]
-VECTOR_ADDS = []
+WIDTH = {"K": 640, "Qa": 1024, "Qb": 1024, "Qc": 512, "V": 512}
+SPLIT = {"K":[320,320,320,320,504],"Qa":[400,552,952,872,736],"Qb":[808,888,904,888,888],"Qc":[512,512,512,512,512],"V":[512,512,512,512,512]}
+TAIL_ON_SCALAR = 5
+X_ON_SCALAR = [[0, 2, 4], [0, 2, 4]]
+ROPES = {"K":[0,0,0,0,0],"xt":[0,0],"x":[0,0],"Qa":[0,1,1,1,1],"Qb":[1,2,2,2,1],"Qc":[1,2,1,4,1],"Vt":[0],"V":[1,1,1,1,0]}
+START = [("w", "K", 0), ("w", "K", 1), ("xt", "xt", 0), ("w", "K", 2), ("x", "x", 0), ("xt", "xt", 1), ("w", "K", 3), ("x", "x", 1), ("w", "K", 4)]
+ADD_ENG = ["vv","vv","vv","gg","gg","gg","gg","gg","gg","gg","gg","vv","vv"]
 RAW_BUFS = 10
 GRP_BUFS = 3
 OUT_BUFS = 3
@@ -55,16 +54,15 @@ def tile_gqattention_pa_kernel(tc, x, cos_f, sin_f, Wq, Wk, Wv, out_0, out_1, ou
         prodp = ctx.enter_context(tc.tile_pool(name="prodp", bufs=PROD_BUFS))
         outp = ctx.enter_context(tc.tile_pool(name="outp", bufs=OUT_BUFS))
         psum = ctx.enter_context(tc.psum_pool(name="psum", bufs=8))
-        ctx.enter_context(tc.manual_schedule())
 
         raws = {}
         loads = []
         for kind, key, g in items:
-            if kind == "x":
+            if kind == "xt":
                 loads.extend([("x", 2 * g), ("x", 2 * g + 1)])
             elif kind == "w":
                 loads.append((key, g))
-        count = {"load": 0, "rope": 0}
+        count = {"load": 0, "rope": 0, "due": 0}
 
         def issue(n):
             for i in range(count["load"], min(count["load"] + n, len(loads))):
@@ -123,19 +121,23 @@ def tile_gqattention_pa_kernel(tc, x, cos_f, sin_f, Wq, Wk, Wv, out_0, out_1, ou
                 codes[key] = (wc, ws)
                 grp = grpp.tile([P, NG, HD, 4], BF16, name="grp", tag="grp", align_bytes=64)
                 for gg in range(NG):
-                    regroup(gg < TAIL_ON_SCALAR[key], grp[:, gg], raws[key[0], gg][:, :, 512:640])
-            else:
-                grp = prodp.tile([P, NG, 256, 4], BF16, name="xg", tag="pr", align_bytes=64)
+                    regroup(gg < TAIL_ON_SCALAR, grp[:, gg], raws["V", gg][:, :, 512:640])
+            elif kind == "xt":
+                grp = []
                 for gg in range(NG):
                     xt = psum.tile([P, 2, 256], F32, name="xt", tag="ps")
+                    grp.append(xt)
                     for u in range(2):
                         for j in range(2):
                             xw = raws["x", 2 * g + j][:].bitcast(F32)
                             nc.tensor.transpose(out=xt[:, u, P * j:P * (j + 1)], in_=xw[:, 256 * gg + u:256 * (gg + 1):2],
                                                 identity=ident[:])
+            else:
+                grp = prodp.tile([P, NG, 256, 4], BF16, name="xg", tag="pr", align_bytes=64)
+                for gg in range(NG):
                     dst = grp[:, gg].rearrange("p s t -> p (s t)").bitcast(F32).rearrange("p (s u) -> p s u", u=2)
-                    src = xt[:].rearrange("p u s -> p s u")
-                    if gg % 2 == 0 and gg // 2 < X_ON_SCALAR[g]:
+                    src = grouped["xt", g][gg][:].rearrange("p u s -> p s u")
+                    if gg in X_ON_SCALAR[g]:
                         nc.scalar.copy(out=dst, in_=src)
                     else:
                         nc.vector.tensor_copy(out=dst, in_=src)
@@ -151,8 +153,11 @@ def tile_gqattention_pa_kernel(tc, x, cos_f, sin_f, Wq, Wk, Wv, out_0, out_1, ou
         def quant_item(kind, key, g):
             if kind == "w":
                 wc, ws = codes[key]
-                nc.vector.quantize_mx(out=wc[:, g, :].bitcast(FP8X4), scales=ws[:, g, :],
-                                      in_=grouped[key, g][:].rearrange("p c t -> p (c t)"))
+                for c0, c1 in ((0, 512), (512, 640)) if key == "K" else ((0, WIDTH[key]),):
+                    nc.vector.quantize_mx(out=wc[:, g, c0:c1].bitcast(FP8X4), scales=ws[:, g, c0:c1],
+                                          in_=grouped[key, g][:, c0:c1, :].rearrange("p c t -> p (c t)"))
+            elif kind == "xt":
+                return
             elif kind == "t":
                 quant5(codes[key][0], codes[key][1], grouped[key, g])
             else:
@@ -189,11 +194,11 @@ def tile_gqattention_pa_kernel(tc, x, cos_f, sin_f, Wq, Wk, Wv, out_0, out_1, ou
             if nchunks == 1:
                 pair_units([accs[t, 0] for t in range(NT)], dram, c0)
 
-        def mm_tail(key):
+        def mm_tail(key, c0):
             acc = psum.tile([P, 512], F32, name="acc", tag="ps")
             for t in range(NT):
                 for g in range(NG):
-                    mx(acc[:, P * t:P * (t + 1)], key, g, t, 0, P)
+                    mx(acc[:, P * t:P * (t + 1)], key, g, t, c0, P)
             return acc
 
         open_acc = {}
@@ -211,10 +216,12 @@ def tile_gqattention_pa_kernel(tc, x, cos_f, sin_f, Wq, Wk, Wv, out_0, out_1, ou
         live = {}
 
         def rope_mults(n):
-            for i in range(n):
+            count["due"] += n
+            for i in range(count["due"]):
                 u, b = count["rope"] // 2, count["rope"] % 2
                 if u >= len(units):
                     return
+                count["due"] -= 1
                 accs, tabs, dram = units[u]
                 nb = len(accs)
                 if b == 0:
@@ -226,9 +233,10 @@ def tile_gqattention_pa_kernel(tc, x, cos_f, sin_f, Wq, Wk, Wv, out_0, out_1, ou
                 count["rope"] += 1 if b + 1 < nb else 2 - b
                 if b + 1 == nb:
                     o = outp.tile([P, nb, 4, HD], F32, name="o", tag="o")
-                    eng = nc.vector if u in VECTOR_ADDS else nc.gpsimd
-                    eng.tensor_tensor(out=o[:, :, :, 0:64], in0=pr[:, :, 0, :, 0:64], in1=pr[:, :, 1, :, 64:128], op=ADD)
-                    eng.tensor_tensor(out=o[:, :, :, 64:128], in0=pr[:, :, 0, :, 64:128], in1=pr[:, :, 1, :, 0:64], op=ADD)
+                    lo_eng = nc.vector if ADD_ENG[u][0] == "v" else nc.gpsimd
+                    hi_eng = nc.vector if ADD_ENG[u][1] == "v" else nc.gpsimd
+                    lo_eng.tensor_tensor(out=o[:, :, :, 0:64], in0=pr[:, :, 0, :, 0:64], in1=pr[:, :, 1, :, 64:128], op=ADD)
+                    hi_eng.tensor_tensor(out=o[:, :, :, 64:128], in0=pr[:, :, 0, :, 64:128], in1=pr[:, :, 1, :, 0:64], op=ADD)
                     nc.sync.dma_start(out=dram, in_=o[:, 0] if nb == 1 else o[:].rearrange("p b h d -> p b (h d)"))
 
         tables()
@@ -246,25 +254,25 @@ def tile_gqattention_pa_kernel(tc, x, cos_f, sin_f, Wq, Wk, Wv, out_0, out_1, ou
                         state["kpass"] = gg + 1
                         if gg == NG - 1:
                             pair_units(open_acc["K"], ok, 0)
-            if key == "Kt":
-                units.append(([mm_tail("Kt")], [tab[:].rearrange("p t r d -> p r t d")], ok[:, :, 512:640]))
+                            units.append(([mm_tail("K", 512)], [tab[:].rearrange("p t r d -> p r t d")], ok[:, :, 512:640]))
             if g == NG - 1 and key in ("Qa", "Qb", "Qc"):
                 mm_group(key, oq, source[key][1])
             if key == "V":
                 mm_pass("V", g)
                 if g == 2:
-                    state["vt"] = mm_tail("Vt")
+                    state["vt"] = mm_tail("Vt", 0)
 
         for i in range(len(items)):
             kind, key, g = items[i]
             copy_item(kind, key, g)
-            issue(2 if kind == "x" else 5 if key == "Kt" else 0 if kind == "t" or key in ("K", "V") else 1)
+            issue(2 if kind == "xt" else 1 if kind == "w" and key != "V" else 0)
             if i > 0:
                 quant_item(*items[i - 1])
             rope_mults(ROPES[key][g])
             if i > 0:
                 after_quant(*items[i - 1])
         quant_item(*items[-1])
+        rope_mults(2 * len(units))
         ot = outp.tile([P, 512], F32, name="o", tag="o")
         nc.scalar.copy(out=ot[:], in_=state["vt"][:])
         nc.sync.dma_start(out=ov[:, :, 512:640], in_=ot[:].rearrange("p (t c) -> p t c", c=P))

@@ -20,7 +20,7 @@ NG = HID // 512
 FLOPS = 2 * TOK * HID * 3840
 
 WIDTH = {"K": 640, "Qa": 1024, "Qb": 1024, "Qc": 512, "V": 512}
-SPLIT = {"K":[320,320,320,320,504],"Qa":[400,552,952,872,736],"Qb":[808,888,904,888,888],"Qc":[512,512,512,512,512],"V":[512,512,512,512,512]}
+SPLIT = {"K":[320,320,320,320,504],"Qa":[336,488,888,808,672],"Qb":[752,832,848,832,832],"Qc":[512,512,512,512,512],"V":[512,512,512,512,512]}
 TAIL_ON_SCALAR = 5
 X_ON_SCALAR = [[0, 2, 4], [0, 2, 4]]
 ROPES = {"K":[0,0,0,0,0],"xt":[0,0],"x":[0,0],"Qa":[0,1,1,1,1],"Qb":[1,2,2,2,1],"Qc":[1,2,1,4,1],"Vt":[0],"V":[1,1,1,1,0]}

@@ -25,11 +25,10 @@ TAIL_ON_SCALAR = 5
 X_ON_SCALAR = [[0, 2, 4], [0, 2, 4]]
 ROPES = {"K":[0,0,0,0,0],"xt":[0,0],"x":[0,0],"Qa":[0,1,1,1,1],"Qb":[1,2,2,2,1],"Qc":[1,2,1,4,1],"Vt":[0],"V":[1,1,1,1,0]}
 START = [("w", "K", 0), ("w", "K", 1), ("xt", "xt", 0), ("w", "K", 2), ("x", "x", 0), ("xt", "xt", 1), ("w", "K", 3), ("x", "x", 1), ("w", "K", 4)]
-ADD_ENG = ["vv","vv","vv","gg","gg","gg","gg","gg","gg","gg","gg","vv","vv"]
 RAW_BUFS = 10
 GRP_BUFS = 3
-OUT_BUFS = 3
-PROD_BUFS = 3
+OUT_BUFS = 4
+PROD_BUFS = 5
 
 
 def tile_gqattention_pa_kernel(tc, x, cos_f, sin_f, Wq, Wk, Wv, out_0, out_1, out_2):
@@ -133,7 +132,7 @@ def tile_gqattention_pa_kernel(tc, x, cos_f, sin_f, Wq, Wk, Wv, out_0, out_1, ou
                             nc.tensor.transpose(out=xt[:, u, P * j:P * (j + 1)], in_=xw[:, 256 * gg + u:256 * (gg + 1):2],
                                                 identity=ident[:])
             else:
-                grp = prodp.tile([P, NG, 256, 4], BF16, name="xg", tag="pr", align_bytes=64)
+                grp = grpp.tile([P, NG, 256, 4], BF16, name="grp", tag="grp", align_bytes=64)
                 for gg in range(NG):
                     dst = grp[:, gg].rearrange("p s t -> p (s t)").bitcast(F32).rearrange("p (s u) -> p s u", u=2)
                     src = grouped["xt", g][gg][:].rearrange("p u s -> p s u")
@@ -215,6 +214,9 @@ def tile_gqattention_pa_kernel(tc, x, cos_f, sin_f, Wq, Wk, Wv, out_0, out_1, ou
 
         live = {}
 
+        def halves(ap):
+            return ap.rearrange("p h (f j) -> p h f j", f=2)
+
         def rope_mults(n):
             count["due"] += n
             for i in range(count["due"]):
@@ -225,18 +227,15 @@ def tile_gqattention_pa_kernel(tc, x, cos_f, sin_f, Wq, Wk, Wv, out_0, out_1, ou
                 accs, tabs, dram = units[u]
                 nb = len(accs)
                 if b == 0:
-                    pr = prodp.tile([P, nb, 2, 4, HD], F32, name="pr", tag="pr", align_bytes=64)
-                    live["pr"] = pr
-                pr = live["pr"]
+                    o = outp.tile([P, nb, 4, HD], F32, name="o", tag="o")
+                    live["o"] = o
+                o = live["o"]
+                pr = prodp.tile([P, 2, 4, HD], F32, name="pr", tag="pr", align_bytes=64)
                 a4 = accs[b][:].rearrange("p (h d) -> p h d", d=HD).unsqueeze(1).to_broadcast([P, 2, 4, HD])
-                nc.vector.tensor_tensor(out=pr[:, b], in0=a4, in1=tabs[b], op=MULT)
+                nc.vector.tensor_tensor(out=pr[:], in0=a4, in1=tabs[b], op=MULT)
+                nc.gpsimd.tensor_tensor(out=halves(o[:, b]), in0=halves(pr[:, 0]), in1=halves(pr[:, 1])[:, :, ::-1, :], op=ADD)
                 count["rope"] += 1 if b + 1 < nb else 2 - b
                 if b + 1 == nb:
-                    o = outp.tile([P, nb, 4, HD], F32, name="o", tag="o")
-                    lo_eng = nc.vector if ADD_ENG[u][0] == "v" else nc.gpsimd
-                    hi_eng = nc.vector if ADD_ENG[u][1] == "v" else nc.gpsimd
-                    lo_eng.tensor_tensor(out=o[:, :, :, 0:64], in0=pr[:, :, 0, :, 0:64], in1=pr[:, :, 1, :, 64:128], op=ADD)
-                    hi_eng.tensor_tensor(out=o[:, :, :, 64:128], in0=pr[:, :, 0, :, 64:128], in1=pr[:, :, 1, :, 0:64], op=ADD)
                     nc.sync.dma_start(out=dram, in_=o[:, 0] if nb == 1 else o[:].rearrange("p b h d -> p b (h d)"))
 
         tables()

@@ -20,7 +20,7 @@ NG = HID // 512
 FLOPS = 2 * TOK * HID * 3840
 
 WIDTH = {"K": 640, "Qa": 1024, "Qb": 1024, "Qc": 512, "V": 512}
-SPLIT = {"K":[320,320,320,320,504],"Qa":[336,488,888,808,672],"Qb":[752,832,848,832,832],"Qc":[512,512,512,512,512],"V":[512,512,512,512,512]}
+SPLIT = {"K":[320,320,320,320,512],"Qa":[336,480,896,816,672],"Qb":[752,832,848,832,832],"Qc":[512,512,512,512,512],"V":[512,512,512,512,512]}
 TAIL_ON_SCALAR = 5
 X_ON_SCALAR = [[0, 2, 4], [0, 2, 4]]
 ROPES = {"K":[0,0,0,0,0],"xt":[0,0],"x":[0,0],"Qa":[0,1,1,1,1],"Qb":[1,2,2,2,1],"Qc":[1,2,1,4,1],"Vt":[0],"V":[1,1,1,1,0]}
@@ -91,8 +91,8 @@ def tile_gqattention_pa_kernel(tc, x, cos_f, sin_f, Wq, Wk, Wv, out_0, out_1, ou
             nc.gpsimd.tensor_scalar(out=tab[:, :, 1, 64:128], in0=cs[:, 1, :, 0:64], scalar1=-1.0, scalar2=0.0, op0=MULT, op1=ADD)
 
         def regroup(on_scalar, dst, src):
-            d = dst.rearrange("p (c i) t -> p c t i", i=4)
-            s = src.rearrange("p t (c i) -> p c t i", i=4)
+            d = dst.rearrange("p (c i) t -> p c t i", i=8)
+            s = src.rearrange("p t (c i) -> p c t i", i=8)
             if on_scalar:
                 nc.scalar.copy(out=d, in_=s)
             else:

@@ -20,10 +20,10 @@ NG = HID // 512
 FLOPS = 2 * TOK * HID * 3840
 
 WIDTH = {"K": 640, "Qa": 1024, "Qb": 1024, "Qc": 512, "V": 512}
-SPLIT = {"K":[320,320,320,320,512],"Qa":[336,480,896,816,672],"Qb":[752,832,848,832,832],"Qc":[512,512,512,512,512],"V":[512,512,512,512,512]}
+SPLIT = {"K": 320, "Qa": 640, "Qb": 816, "Qc": 512, "V": 512}
 TAIL_ON_SCALAR = 5
 X_ON_SCALAR = [[0, 2, 4], [0, 2, 4]]
-ROPES = {"K":[0,0,0,0,0],"xt":[0,0],"x":[0,0],"Qa":[0,1,1,1,1],"Qb":[1,2,2,2,1],"Qc":[1,2,1,4,1],"Vt":[0],"V":[1,1,1,1,0]}
+ROPES = 2
 START = [("w", "K", 0), ("w", "K", 1), ("xt", "xt", 0), ("w", "K", 2), ("x", "x", 0), ("xt", "xt", 1), ("w", "K", 3), ("x", "x", 1), ("w", "K", 4)]
 RAW_BUFS = 10
 GRP_BUFS = 3
@@ -109,7 +109,7 @@ def tile_gqattention_pa_kernel(tc, x, cos_f, sin_f, Wq, Wk, Wv, out_0, out_1, ou
                     ws = codep.tile([P, NG, w], U8, name="ws", tag="ws", align_bytes=64)
                     codes[key] = (wc, ws)
                 grp = grpp.tile([P, w, 4], BF16, name="grp", tag="grp", align_bytes=64)
-                c = SPLIT[key][g]
+                c = SPLIT[key]
                 raw = raws[key, g]
                 regroup(True, grp[:, 0:c, :], raw[:, :, 0:c])
                 if c < w:
@@ -218,12 +218,10 @@ def tile_gqattention_pa_kernel(tc, x, cos_f, sin_f, Wq, Wk, Wv, out_0, out_1, ou
             return ap.rearrange("p h (f j) -> p h f j", f=2)
 
         def rope_mults(n):
-            count["due"] += n
-            for i in range(count["due"]):
+            for i in range(n):
                 u, b = count["rope"] // 2, count["rope"] % 2
                 if u >= len(units):
                     return
-                count["due"] -= 1
                 accs, tabs, dram = units[u]
                 nb = len(accs)
                 if b == 0:
@@ -267,7 +265,7 @@ def tile_gqattention_pa_kernel(tc, x, cos_f, sin_f, Wq, Wk, Wv, out_0, out_1, ou
             issue(2 if kind == "xt" else 1 if kind == "w" and key != "V" else 0)
             if i > 0:
                 quant_item(*items[i - 1])
-            rope_mults(ROPES[key][g])
+            rope_mults(ROPES)
             if i > 0:
                 after_quant(*items[i - 1])
         quant_item(*items[-1])

from contextlib import ExitStack

import concourse.mybir as mybir
from concourse.masks import make_identity

F32 = mybir.dt.float32
BF16 = mybir.dt.bfloat16
U32 = mybir.dt.uint32
U8 = mybir.dt.uint8
FP8X4 = mybir.dt.float8_e4m3fn_x4
MULT = mybir.AluOpType.mult
ADD = mybir.AluOpType.add

P = 128
TOK = 512
HID = 2560
HD = 128
NT = TOK // P
NG = HID // 512
FLOPS = 2 * TOK * HID * 3840

WIDTH = {"K": 640, "Qa": 1024, "Qb": 1024, "Qc": 512, "V": 512}
SPLIT = {"K": 320, "Qa": 640, "Qb": 816, "Qc": 512, "V": 512}
TAIL_ON_SCALAR = 5
X_ON_SCALAR = [[0, 2, 4], [0, 2, 4]]
ROPES = 2
START = [("w", "K", 0), ("w", "K", 1), ("xt", "xt", 0), ("w", "K", 2), ("x", "x", 0), ("xt", "xt", 1), ("w", "K", 3), ("x", "x", 1), ("w", "K", 4)]
RAW_BUFS = 10
GRP_BUFS = 3
OUT_BUFS = 4
PROD_BUFS = 5


def tile_gqattention_pa_kernel(tc, x, cos_f, sin_f, Wq, Wk, Wv, out_0, out_1, out_2):
    nc = tc.nc
    x2 = x.flatten_outer_dims().rearrange("(p t) k -> p t k", t=NT)
    oq = out_0.rearrange("b s h d -> (b s) (h d)").rearrange("(p t) c -> p t c", t=NT)
    ok = out_1.rearrange("b s h d -> (b s) (h d)").rearrange("(p t) c -> p t c", t=NT)
    ov = out_2.rearrange("b s h d -> (b s) (h d)").rearrange("(p t) c -> p t c", t=NT)
    source = {"K": (Wk, 0, 640), "Qa": (Wq, 0, 1024), "Qb": (Wq, 1024, 1024), "Qc": (Wq, 2048, 512), "V": (Wv, 0, 640)}

    items = list(START)
    for key in ("Qa", "Qb", "Qc"):
        items.extend([("w", key, g) for g in range(NG)])
    items.append(("t", "Vt", 0))
    items.extend([("w", "V", g) for g in range(NG)])

    with ExitStack() as ctx:
        const = ctx.enter_context(tc.tile_pool(name="const", bufs=1))
        rawp = ctx.enter_context(tc.tile_pool(name="rawp", bufs=RAW_BUFS))
        grpp = ctx.enter_context(tc.tile_pool(name="grpp", bufs=GRP_BUFS))
        codep = ctx.enter_context(tc.tile_pool(name="codep", bufs=2))
        prodp = ctx.enter_context(tc.tile_pool(name="prodp", bufs=PROD_BUFS))
        outp = ctx.enter_context(tc.tile_pool(name="outp", bufs=OUT_BUFS))
        psum = ctx.enter_context(tc.psum_pool(name="psum", bufs=8))

        raws = {}
        loads = []
        for kind, key, g in items:
            if kind == "xt":
                loads.extend([("x", 2 * g), ("x", 2 * g + 1)])
            elif kind == "w":
                loads.append((key, g))
        count = {"load": 0, "rope": 0, "due": 0}

        def issue(n):
            for i in range(count["load"], min(count["load"] + n, len(loads))):
                key, g = loads[i]
                if key == "x":
                    t = rawp.tile([P, HID], BF16, name="xraw", tag="raw")
                    nc.sync.dma_start(out=t[:], in_=x2[:, g, :])
                else:
                    src, c0, w = source[key]
                    t = rawp.tile([P, 4, w], BF16, name="raw", tag="raw")
                    nc.sync.dma_start(out=t[:], in_=src[512 * g:512 * (g + 1), c0:c0 + w].rearrange("(p t) c -> p t c", t=4))
                raws[key, g] = t
            count["load"] = min(count["load"] + n, len(loads))

        ident = const.tile([P, P], F32, name="ident")
        make_identity(nc, ident[:])
        cs = const.tile([P, 2, NT, HD], BF16, name="cs")
        tab = const.tile([P, NT, 2, HD], F32, name="tab")
        xc = const.tile([P, 2, NG, 256], U32, name="xc", align_bytes=64)
        xs = const.tile([P, 2, NG, 256], U8, name="xs", align_bytes=64)

        def tables():
            nc.scalar.dma_start(out=cs[:, 0], in_=cos_f.rearrange("(p t) d -> p t d", t=NT))
            nc.scalar.dma_start(out=cs[:, 1], in_=sin_f.rearrange("(p t) d -> p t d", t=NT))
            nc.gpsimd.tensor_scalar(out=tab[:, :, 0, :], in0=cs[:, 0], scalar1=1.0, scalar2=0.0, op0=MULT, op1=ADD)
            nc.gpsimd.tensor_scalar(out=tab[:, :, 1, 0:64], in0=cs[:, 1, :, 64:128], scalar1=1.0, scalar2=0.0, op0=MULT, op1=ADD)
            nc.gpsimd.tensor_scalar(out=tab[:, :, 1, 64:128], in0=cs[:, 1, :, 0:64], scalar1=-1.0, scalar2=0.0, op0=MULT, op1=ADD)

        def regroup(on_scalar, dst, src):
            d = dst.rearrange("p (c i) t -> p c t i", i=8)
            s = src.rearrange("p t (c i) -> p c t i", i=8)
            if on_scalar:
                nc.scalar.copy(out=d, in_=s)
            else:
                nc.vector.tensor_copy(out=d, in_=s)

        codes = {}
        grouped = {}

        def copy_item(kind, key, g):
            if kind == "w":
                w = WIDTH[key]
                if g == 0:
                    wc = codep.tile([P, NG, w], U32, name="wc", tag="wc", align_bytes=64)
                    ws = codep.tile([P, NG, w], U8, name="ws", tag="ws", align_bytes=64)
                    codes[key] = (wc, ws)
                grp = grpp.tile([P, w, 4], BF16, name="grp", tag="grp", align_bytes=64)
                c = SPLIT[key]
                raw = raws[key, g]
                regroup(True, grp[:, 0:c, :], raw[:, :, 0:c])
                if c < w:
                    regroup(False, grp[:, c:w, :], raw[:, :, c:w])
            elif kind == "t":
                wc = codep.tile([P, NG, HD], U32, name="tc", tag="tc", align_bytes=64)
                ws = codep.tile([P, NG, HD], U8, name="tsc", tag="tsc", align_bytes=64)
                codes[key] = (wc, ws)
                grp = grpp.tile([P, NG, HD, 4], BF16, name="grp", tag="grp", align_bytes=64)
                for gg in range(NG):
                    regroup(gg < TAIL_ON_SCALAR, grp[:, gg], raws["V", gg][:, :, 512:640])
            elif kind == "xt":
                grp = []
                for gg in range(NG):
                    xt = psum.tile([P, 2, 256], F32, name="xt", tag="ps")
                    grp.append(xt)
                    for u in range(2):
                        for j in range(2):
                            xw = raws["x", 2 * g + j][:].bitcast(F32)
                            nc.tensor.transpose(out=xt[:, u, P * j:P * (j + 1)], in_=xw[:, 256 * gg + u:256 * (gg + 1):2],
                                                identity=ident[:])
            else:
                grp = grpp.tile([P, NG, 256, 4], BF16, name="grp", tag="grp", align_bytes=64)
                for gg in range(NG):
                    dst = grp[:, gg].rearrange("p s t -> p (s t)").bitcast(F32).rearrange("p (s u) -> p s u", u=2)
                    src = grouped["xt", g][gg][:].rearrange("p u s -> p s u")
                    if gg in X_ON_SCALAR[g]:
                        nc.scalar.copy(out=dst, in_=src)
                    else:
                        nc.vector.tensor_copy(out=dst, in_=src)
            grouped[key, g] = grp

        def quant5(dst_c, dst_s, src):
            nc.vector.quantize_mx(out=dst_c[:, 0:4, :].rearrange("p g c -> p (g c)").bitcast(FP8X4),
                                  scales=dst_s[:, 0:4, :].rearrange("p g c -> p (g c)"),
                                  in_=src[:, 0:4].rearrange("p g c t -> p (g c t)"))
            nc.vector.quantize_mx(out=dst_c[:, 4, :].bitcast(FP8X4), scales=dst_s[:, 4, :],
                                  in_=src[:, 4].rearrange("p c t -> p (c t)"))

        def quant_item(kind, key, g):
            if kind == "w":
                wc, ws = codes[key]
                for c0, c1 in ((0, 512), (512, 640)) if key == "K" else ((0, WIDTH[key]),):
                    nc.vector.quantize_mx(out=wc[:, g, c0:c1].bitcast(FP8X4), scales=ws[:, g, c0:c1],
                                          in_=grouped[key, g][:, c0:c1, :].rearrange("p c t -> p (c t)"))
            elif kind == "xt":
                return
            elif kind == "t":
                quant5(codes[key][0], codes[key][1], grouped[key, g])
            else:
                quant5(xc[:, g], xs[:, g], grouped[key, g])

        def mx(acc, key, g, t, c0, n):
            wc, ws = codes[key]
            tok = slice(P * (t % 2), P * (t % 2) + P)
            nc.tensor.matmul_mx(out=acc, lhsT=xc[:, t // 2, g, tok].bitcast(FP8X4), lhsT_scale=xs[:, t // 2, g, tok],
                                rhs=wc[:, g, c0:c0 + n].bitcast(FP8X4), rhs_scale=ws[:, g, c0:c0 + n],
                                start=(g == 0), stop=(g == NG - 1))

        units = []

        def tab_of(t):
            return tab[:, t].unsqueeze(2).to_broadcast([P, 2, 4, HD])

        def pair_units(accs, dram, c0):
            for t in (0, 2):
                units.append(([accs[t], accs[t + 1]], [tab_of(t), tab_of(t + 1)], dram[:, t:t + 2, c0:c0 + 512]))

        def mm_group(key, dram, c0):
            accs = {}
            nchunks = WIDTH[key] // 512
            for t in range(NT):
                for c in range(nchunks):
                    acc = psum.tile([P, 512], F32, name="acc", tag="ps")
                    accs[t, c] = acc
                    for g in range(NG):
                        mx(acc[:], key, g, t, 512 * c, 512)
                if nchunks == 2:
                    units.append(([accs[t, 0], accs[t, 1]], [tab_of(t), tab_of(t)],
                                  dram[:, t, c0:c0 + 1024].rearrange("p (b c) -> p b c", b=2)))
            if nchunks == 1:
                pair_units([accs[t, 0] for t in range(NT)], dram, c0)

        def mm_tail(key, c0):
            acc = psum.tile([P, 512], F32, name="acc", tag="ps")
            for t in range(NT):
                for g in range(NG):
                    mx(acc[:, P * t:P * (t + 1)], key, g, t, c0, P)
            return acc

        open_acc = {}

        def mm_pass(key, g):
            if g == 0:
                accs = []
                for t in range(NT):
                    acc = psum.tile([P, 512], F32, name="acc", tag="ps")
                    accs.append(acc)
                open_acc[key] = accs
            for t in range(NT):
                mx(open_acc[key][t][:], key, g, t, 0, 512)

        live = {}

        def halves(ap):
            return ap.rearrange("p h (f j) -> p h f j", f=2)

        def rope_mults(n):
            for i in range(n):
                u, b = count["rope"] // 2, count["rope"] % 2
                if u >= len(units):
                    return
                accs, tabs, dram = units[u]
                nb = len(accs)
                if b == 0:
                    o = outp.tile([P, nb, 4, HD], F32, name="o", tag="o")
                    live["o"] = o
                o = live["o"]
                pr = prodp.tile([P, 2, 4, HD], F32, name="pr", tag="pr", align_bytes=64)
                a4 = accs[b][:].rearrange("p (h d) -> p h d", d=HD).unsqueeze(1).to_broadcast([P, 2, 4, HD])
                nc.vector.tensor_tensor(out=pr[:], in0=a4, in1=tabs[b], op=MULT)
                nc.gpsimd.tensor_tensor(out=halves(o[:, b]), in0=halves(pr[:, 0]), in1=halves(pr[:, 1])[:, :, ::-1, :], op=ADD)
                count["rope"] += 1 if b + 1 < nb else 2 - b
                if b + 1 == nb:
                    nc.sync.dma_start(out=dram, in_=o[:, 0] if nb == 1 else o[:].rearrange("p b h d -> p b (h d)"))

        tables()
        issue(RAW_BUFS)
        done = set()
        state = {"kpass": 0, "vt": None}

        def after_quant(kind, key, g):
            done.add((key, g))
            x_ready = ("x", 0) in done and ("x", 1) in done
            if x_ready:
                for gg in range(state["kpass"], NG):
                    if ("K", gg) in done and state["kpass"] == gg:
                        mm_pass("K", gg)
                        state["kpass"] = gg + 1
                        if gg == NG - 1:
                            pair_units(open_acc["K"], ok, 0)
                            units.append(([mm_tail("K", 512)], [tab[:].rearrange("p t r d -> p r t d")], ok[:, :, 512:640]))
            if g == NG - 1 and key in ("Qa", "Qb", "Qc"):
                mm_group(key, oq, source[key][1])
            if key == "V":
                mm_pass("V", g)
                if g == 2:
                    state["vt"] = mm_tail("Vt", 0)

        for i in range(len(items)):
            kind, key, g = items[i]
            copy_item(kind, key, g)
            issue(2 if kind == "xt" else 1 if kind == "w" and key != "V" else 0)
            if i > 0:
                quant_item(*items[i - 1])
            rope_mults(ROPES)
            if i > 0:
                after_quant(*items[i - 1])
        quant_item(*items[-1])
        rope_mults(2 * len(units))
        ot = outp.tile([P, 512], F32, name="o", tag="o")
        nc.scalar.copy(out=ot[:], in_=state["vt"][:])
        nc.sync.dma_start(out=ov[:, :, 512:640], in_=ot[:].rearrange("p (t c) -> p t c", c=P))
        after_quant(*items[-1])
        for t in range(NT):
            o1 = outp.tile([P, 512], F32, name="o1", tag="o1", bufs=4)
            if t % 2 == 0:
                nc.scalar.copy(out=o1[:], in_=open_acc["V"][t][:])
            else:
                nc.vector.tensor_copy(out=o1[:], in_=open_acc["V"][t][:])
            nc.sync.dma_start(out=ov[:, t, 0:512], in_=o1[:])
